import numpy as np
import ml_dtypes


def mxq(x, axis, fmt="e4m3"):
    dtype, down = {"e4m3": (ml_dtypes.float8_e4m3fn, 7), "e5m2": (ml_dtypes.float8_e5m2, 14)}[fmt]
    v = np.moveaxis(np.asarray(x, np.float32).astype(ml_dtypes.bfloat16).astype(np.float64), axis, -1)
    blocks = v.reshape(v.shape[:-1] + (-1, 32))
    amax = np.abs(blocks).max(-1, keepdims=True)
    byte = np.maximum(np.where(amax > 0, np.frexp(amax)[1] - 1 + 127, 0) - down, 1)
    scale = np.exp2(byte - 127.0)
    codes = (blocks / scale).astype(np.float32).astype(dtype).astype(np.float64)
    return np.moveaxis((codes * scale).reshape(v.shape), -1, axis)


WIDE = False


def mx_kscale(k):
    if not WIDE:
        return np.ones(k)
    levels = np.array([10, -10, 5, -5, 0])
    a = np.random.permutation(np.resize(levels, k // 512 * 4)).reshape(k // 512, 4)
    idx = np.arange(k)
    return np.exp2(a[idx // 512, idx % 128 // 32])


BF16 = ml_dtypes.bfloat16


def bf(x):
    return np.asarray(x, np.float32).astype(BF16)


def f64(x):
    return np.asarray(x).astype(np.float64)


E2M1 = np.array([0.0, 0.5, 1.0, 1.5, 2.0, 3.0, 4.0, 6.0, -0.0, -0.5, -1.0, -1.5, -2.0, -3.0, -4.0, -6.0])


def pack_weight(w, fmt):
    k, n = w.shape
    w = f64(bf(w)).reshape(k // 32, 32, n)
    amax = np.abs(w).max(1)
    if fmt == "e4m3":
        byte = np.frexp(amax)[1] - 1 + 127 - 7
    else:
        mant, ex = np.frexp(amax / 6.0)
        byte = np.where(mant > 0.5, ex, ex - 1) + 127
    byte = np.clip(np.where(amax > 0, byte, 1), 1, 254)
    scaled = (w * np.exp2(127.0 - byte)[:, None, :]).reshape(k, n).astype(np.float32)
    by_word = np.ascontiguousarray(scaled.reshape(k // 512, 128, 4, n).transpose(0, 1, 3, 2))
    if fmt == "e4m3":
        words = by_word.astype(ml_dtypes.float8_e4m3fn).view(np.uint8)
    else:
        c = by_word.astype(ml_dtypes.float4_e2m1fn).view(np.uint8) & 0xF
        words = c[..., 0::2] | (c[..., 1::2] << 4)
    return np.ascontiguousarray(words), np.ascontiguousarray(byte.astype(np.uint8).reshape(k // 512, 16, n))


def unpack_weight(words, scales, fmt):
    g, p, n, _ = words.shape
    if fmt == "e4m3":
        vals = np.ascontiguousarray(words).view(ml_dtypes.float8_e4m3fn).astype(np.float64)
    else:
        nib = np.empty((g, p, n, 4), np.uint8)
        nib[..., 0::2] = words & 0xF
        nib[..., 1::2] = words >> 4
        vals = E2M1[nib]
    vals = vals * np.repeat(np.exp2(scales.astype(np.float64) - 127.0), 8, axis=1)[..., None]
    return vals.transpose(0, 1, 3, 2).reshape(g * 512, n)

def pack4(w):
    words, scales = pack_weight(w, "e2m1")
    return words.reshape(words.shape[0], 128, -1), scales


def unpack4(words, scales):
    return unpack_weight(words.reshape(words.shape[0], 128, -1, 2), scales, "e2m1")


B, S, E, H, DH, ROT, MP = 2, 512, 1024, 8, 128, 32, 4
HD = H * DH
LOC = HD // MP


def rope_sincos():
    inv_freq = 1.0 / (10000.0 ** (np.arange(0, ROT, 2) / ROT))
    ang = np.arange(S)[:, None] * inv_freq[None, :]
    return np.sin(ang), np.cos(ang)


def apply_rope(x, sin, cos):
    sin2 = np.repeat(sin, 2, axis=-1)[None, :, None, :]
    cos2 = np.repeat(cos, 2, axis=-1)[None, :, None, :]
    x1 = x[..., ::2]
    x2 = x[..., 1::2]
    rot = np.stack((-x2, x1), axis=-1).reshape(x.shape)
    return x * cos2 + rot * sin2


def setup_inputs():
    s = mx_kscale(E)
    hidden_states = bf(np.random.standard_normal((B, S, E)) * s)
    w = np.random.standard_normal((3 * HD, E)) / np.sqrt(E) / s[None, :]
    words, scales = pack4(np.ascontiguousarray(w.T))
    return {"hidden_states": hidden_states,
            "W_qkv_words": words,
            "W_qkv_scales": scales}


def reference(hidden_states, W_qkv_words, W_qkv_scales):
    qkv = mxq(f64(hidden_states), 2, "e4m3") @ unpack4(W_qkv_words, W_qkv_scales)
    qkv = qkv.reshape(B, S, MP, 3 * LOC)
    q, k, v = np.split(qkv, 3, axis=-1)
    q = q.reshape(B, S, H, DH)
    k = k.reshape(B, S, H, DH)
    v = v.reshape(B, S, H, DH)
    sin, cos = rope_sincos()
    q = np.concatenate([apply_rope(q[..., :ROT], sin, cos), q[..., ROT:]], axis=-1)
    k = np.concatenate([apply_rope(k[..., :ROT], sin, cos), k[..., ROT:]], axis=-1)
    return q, k, v

@@ -1,0 +1,215 @@
+import math
+
+import concourse.mybir as mybir
+from concourse.masks import make_identity
+
+F32 = mybir.dt.float32
+BF16 = mybir.dt.bfloat16
+I32 = mybir.dt.int32
+U32 = mybir.dt.uint32
+U8 = mybir.dt.uint8
+FP8X4 = mybir.dt.float8_e4m3fn_x4
+FP4X4 = mybir.dt.float4_e2m1fn_x4
+ALU = mybir.AluOpType
+SIN = mybir.ActivationFunctionType.Sin
+
+P = 128
+PACK = 4
+TOKENS = 1024
+POSITIONS = 512
+FEATURES = 1024
+PASSES = FEATURES // (P * PACK)
+TILES = TOKENS // P
+OUTPUTS = 3
+ROTATED = 2
+WIDTH = 1024
+GROUPS = 4
+GROUP_COLS = WIDTH // GROUPS
+BANK = 512
+HALVES = WIDTH // BANK
+HEADS = 8
+HEAD = 128
+ROT = 32
+PAIRS = ROT // 2
+WORDS = FEATURES // 2
+PASS_WORDS = WORDS // PASSES
+ROUND_MAGIC = 12582912.0
+
+FLOPS = 2 * TOKENS * FEATURES * OUTPUTS * WIDTH
+
+
+def tile_progenattention_pa_kernel(
+    tc, hidden_states, W_qkv_words, W_qkv_scales, out_0, out_1, out_2
+):
+    nc = tc.nc
+    x_hbm = hidden_states.rearrange("b (q t) e -> (b q) t e", t=TILES)
+    out_hbm = [
+        o.rearrange("b (q t) h d -> (b q) t (h d)", t=TILES) for o in (out_0, out_1, out_2)
+    ]
+
+    with tc.manual_schedule(), tc.tile_pool(name="keep", bufs=1) as keep, tc.tile_pool(
+        name="grouped_pool", bufs=4
+    ) as grouped_pool, tc.tile_pool(name="result_pool", bufs=4) as result_pool, tc.tile_pool(
+        name="swap_pool", bufs=2
+    ) as swap_pool, tc.psum_pool(name="turned_pool", bufs=2) as turned_pool, tc.psum_pool(
+        name="product_pool", bufs=6
+    ) as product_pool:
+        x_sb = keep.tile([P, TILES, FEATURES], BF16)
+        x_codes = keep.tile([P, TILES, PASSES, P], U32, align_bytes=64)
+        x_scales = keep.tile([P, TILES, PASSES, P], U8, align_bytes=64)
+        w_words = keep.tile([P, PASSES, OUTPUTS, 2 * WIDTH], U8, align_bytes=64)
+        w_scales = keep.tile([P, PASSES, OUTPUTS, WIDTH], U8, align_bytes=64)
+        w_scales_raw = keep.tile([P, PASSES, OUTPUTS * WIDTH], U8)
+        identity = keep.tile([P, P], F32)
+
+        nc.scalar.dma_start(out=x_sb[:, 0:2, :], in_=x_hbm[:, 0:2, :])
+
+        nc.vector.memset(w_scales_raw[:].bitcast(I32), 0)
+        for quadrant in range(4):
+            nc.sync.dma_start(
+                out=w_scales_raw[32 * quadrant : 32 * quadrant + 4, :, :].bitcast(I32),
+                in_=W_qkv_scales[:, 4 * quadrant : 4 * quadrant + 4, :]
+                .bitcast(I32)
+                .rearrange("g r n -> r g n"),
+            )
+        for o in range(OUTPUTS):
+            for g in range(PASSES):
+                nc.sync.dma_start(
+                    out=w_words[:, g, o, :].bitcast(I32).rearrange("p (m c) -> p m c", m=GROUPS),
+                    in_=W_qkv_words[g]
+                    .bitcast(I32)
+                    .rearrange("p (m o c) -> p m o c", m=GROUPS, o=OUTPUTS)[:, :, o, :],
+                )
+        for t in range(2, TILES, 2):
+            nc.sync.dma_start(out=x_sb[:, t : t + 2, :], in_=x_hbm[:, t : t + 2, :])
+
+        make_identity(nc, identity[:])
+        position_int = keep.tile([P, TILES], I32)
+        nc.gpsimd.iota(position_int[:], pattern=[[1, TILES]], base=0, channel_multiplier=TILES)
+        nc.vector.tensor_single_scalar(
+            out=position_int[:], in_=position_int[:], scalar=POSITIONS - 1, op=ALU.bitwise_and
+        )
+        position = keep.tile([P, TILES], F32)
+        nc.vector.tensor_copy(out=position[:], in_=position_int[:])
+        turns = keep.tile([P, TILES, PAIRS], F32)
+        for j in range(PAIRS):
+            nc.vector.tensor_scalar_mul(
+                out=turns[:, :, j],
+                in0=position[:],
+                scalar1=10000.0 ** (-j / PAIRS) / (2.0 * math.pi),
+            )
+        whole = keep.tile([P, TILES, PAIRS], F32)
+        nc.vector.tensor_scalar(
+            out=whole[:],
+            in0=turns[:],
+            scalar1=ROUND_MAGIC,
+            scalar2=ROUND_MAGIC,
+            op0=ALU.add,
+            op1=ALU.subtract,
+        )
+        part = keep.tile([P, TILES, PAIRS], F32)
+        nc.vector.tensor_sub(out=part[:], in0=turns[:], in1=whole[:])
+        quarter_less = keep.tile([P, TILES, PAIRS], F32)
+        nc.vector.scalar_tensor_tensor(
+            out=quarter_less[:], in0=part[:], scalar=-1.0, in1=part[:], op0=ALU.mult, op1=ALU.min
+        )
+        nc.vector.tensor_scalar_add(out=quarter_less[:], in0=quarter_less[:], scalar1=0.25)
+        sin_signed = keep.tile([P, TILES, 2, PAIRS], F32)
+        cos_twice = keep.tile([P, TILES, PAIRS, 2], F32)
+        nc.scalar.activation(
+            out=sin_signed[:, :, 0, :], in_=part[:], func=SIN, scale=-2.0 * math.pi
+        )
+        nc.scalar.activation(
+            out=sin_signed[:, :, 1, :], in_=part[:], func=SIN, scale=2.0 * math.pi
+        )
+        nc.scalar.activation(
+            out=cos_twice[:],
+            in_=quarter_less[:].unsqueeze(3).to_broadcast([P, TILES, PAIRS, 2]),
+            func=SIN,
+            scale=2.0 * math.pi,
+        )
+
+        for o in range(OUTPUTS):
+            nc.vector.tensor_copy(
+                out=w_scales[:, :, o, :].bitcast(I32).rearrange("p g (m c) -> p g m c", m=GROUPS),
+                in_=w_scales_raw[:]
+                .bitcast(I32)
+                .rearrange("p g (m o c) -> p g m o c", m=GROUPS, o=OUTPUTS)[:, :, :, o, :],
+            )
+
+        x_words = x_sb[:].bitcast(F32)
+
+        def quantise_two_tiles(first):
+            grouped_tiles = []
+            for t in (first, first + 1):
+                turned = turned_pool.tile([P, PASSES * 2, P], F32)
+                for g in range(PASSES):
+                    for u in range(2):
+                        nc.tensor.transpose(
+                            turned[:, 2 * g + u, :],
+                            x_words[:, t, PASS_WORDS * g + u : PASS_WORDS * (g + 1) : 2],
+                            identity[:],
+                        )
+                grouped = grouped_pool.tile([P, PASSES, P, PACK], BF16, align_bytes=64)
+                nc.vector.tensor_copy(
+                    out=grouped[:].bitcast(F32),
+                    in_=turned[:].rearrange("p (g u) r -> p g r u", u=2),
+                )
+                grouped_tiles.append(grouped)
+            for t, grouped in zip((first, first + 1), grouped_tiles):
+                nc.vector.quantize_mx(
+                    out=x_codes[:, t].rearrange("p g r -> p (g r)").bitcast(FP8X4),
+                    scales=x_scales[:, t].rearrange("p g r -> p (g r)"),
+                    in_=grouped[:].rearrange("p g r j -> p (g r j)"),
+                )
+
+        def rotate(heads, t):
+            front = heads[:, :, 0:ROT]
+            swapped = swap_pool.tile([P, HEADS, 2, PAIRS], F32)
+            for e in range(2):
+                nc.vector.tensor_tensor(
+                    out=swapped[:, :, e, :],
+                    in0=heads[:, :, 1 - e : ROT : 2],
+                    in1=sin_signed[:, t, e, :].unsqueeze(1).to_broadcast([P, HEADS, PAIRS]),
+                    op=ALU.mult,
+                )
+            nc.vector.tensor_tensor(
+                out=front,
+                in0=front,
+                in1=cos_twice[:, t]
+                .rearrange("p j e -> p (j e)")
+                .unsqueeze(1)
+                .to_broadcast([P, HEADS, ROT]),
+                op=ALU.mult,
+            )
+            pairs = front.rearrange("p h (j e) -> p h j e", e=2)
+            nc.vector.tensor_tensor(
+                out=pairs, in0=pairs, in1=swapped[:].rearrange("p h e j -> p h j e"), op=ALU.add
+            )
+
+        quantise_two_tiles(0)
+        for t in range(TILES):
+            result = result_pool.tile([P, OUTPUTS, WIDTH], F32)
+            for o in range(OUTPUTS):
+                for half in range(HALVES):
+                    product = product_pool.tile([P, BANK], F32)
+                    for g in range(PASSES):
+                        nc.tensor.matmul_mx(
+                            out=product[:],
+                            lhsT=x_codes[:, t, g, :].bitcast(FP8X4),
+                            lhsT_scale=x_scales[:, t, g, :],
+                            rhs=w_words[:, g, o, 2 * BANK * half : 2 * BANK * (half + 1)].bitcast(
+                                FP4X4
+                            ),
+                            rhs_scale=w_scales[:, g, o, BANK * half : BANK * (half + 1)],
+                            start=(g == 0),
+                            stop=(g == PASSES - 1),
+                        )
+                    nc.scalar.copy(
+                        out=result[:, o, BANK * half : BANK * (half + 1)], in_=product[:]
+                    )
+                if o < ROTATED:
+                    rotate(result[:, o, :].rearrange("p (h d) -> p h d", d=HEAD), t)
+                nc.sync.dma_start(out=out_hbm[o][:, t, :], in_=result[:, o, :])
+            if t % 2 == 0 and t + 2 < TILES:
+                quantise_two_tiles(t + 2)

@@ -62,8 +62,22 @@ def tile_progenattention_pa_kernel(
         w_scales_raw = keep.tile([P, PASSES, OUTPUTS * WIDTH], U8)
         identity = keep.tile([P, P], F32)
 
-        nc.scalar.dma_start(out=x_sb[:, 0:2, :], in_=x_hbm[:, 0:2, :])
+        def load_x(first, count, queue):
+            queue.dma_start(
+                out=x_sb[:, first : first + count, :], in_=x_hbm[:, first : first + count, :]
+            )
 
+        def load_w_words(o):
+            for g in range(PASSES):
+                nc.sync.dma_start(
+                    out=w_words[:, g, o, :].bitcast(I32).rearrange("p (m c) -> p m c", m=GROUPS),
+                    in_=W_qkv_words[g]
+                    .bitcast(I32)
+                    .rearrange("p (m o c) -> p m o c", m=GROUPS, o=OUTPUTS)[:, :, o, :],
+                )
+
+        load_x(0, 1, nc.scalar)
+        load_x(1, 1, nc.scalar)
         nc.vector.memset(w_scales_raw[:].bitcast(I32), 0)
         for quadrant in range(4):
             nc.sync.dma_start(
@@ -72,20 +86,16 @@ def tile_progenattention_pa_kernel(
                 .bitcast(I32)
                 .rearrange("g r n -> r g n"),
             )
-        for o in range(OUTPUTS):
-            for g in range(PASSES):
-                nc.sync.dma_start(
-                    out=w_words[:, g, o, :].bitcast(I32).rearrange("p (m c) -> p m c", m=GROUPS),
-                    in_=W_qkv_words[g]
-                    .bitcast(I32)
-                    .rearrange("p (m o c) -> p m o c", m=GROUPS, o=OUTPUTS)[:, :, o, :],
-                )
-        for t in range(2, TILES, 2):
-            nc.sync.dma_start(out=x_sb[:, t : t + 2, :], in_=x_hbm[:, t : t + 2, :])
+        load_w_words(0)
+        load_w_words(1)
+        load_x(2, 2, nc.sync)
+        load_w_words(2)
+        load_x(4, 2, nc.sync)
+        load_x(6, 2, nc.sync)
 
-        make_identity(nc, identity[:])
         position_int = keep.tile([P, TILES], I32)
         nc.gpsimd.iota(position_int[:], pattern=[[1, TILES]], base=0, channel_multiplier=TILES)
+        make_identity(nc, identity[:])
         nc.vector.tensor_single_scalar(
             out=position_int[:], in_=position_int[:], scalar=POSITIONS - 1, op=ALU.bitwise_and
         )
@@ -129,7 +139,7 @@ def tile_progenattention_pa_kernel(
             scale=2.0 * math.pi,
         )
 
-        for o in range(OUTPUTS):
+        def move_w_scales(o):
             nc.vector.tensor_copy(
                 out=w_scales[:, :, o, :].bitcast(I32).rearrange("p g (m c) -> p g m c", m=GROUPS),
                 in_=w_scales_raw[:]
@@ -139,29 +149,28 @@ def tile_progenattention_pa_kernel(
 
         x_words = x_sb[:].bitcast(F32)
 
-        def quantise_two_tiles(first):
-            grouped_tiles = []
-            for t in (first, first + 1):
-                turned = turned_pool.tile([P, PASSES * 2, P], F32)
-                for g in range(PASSES):
-                    for u in range(2):
-                        nc.tensor.transpose(
-                            turned[:, 2 * g + u, :],
-                            x_words[:, t, PASS_WORDS * g + u : PASS_WORDS * (g + 1) : 2],
-                            identity[:],
-                        )
-                grouped = grouped_pool.tile([P, PASSES, P, PACK], BF16, align_bytes=64)
-                nc.vector.tensor_copy(
-                    out=grouped[:].bitcast(F32),
-                    in_=turned[:].rearrange("p (g u) r -> p g r u", u=2),
-                )
-                grouped_tiles.append(grouped)
-            for t, grouped in zip((first, first + 1), grouped_tiles):
-                nc.vector.quantize_mx(
-                    out=x_codes[:, t].rearrange("p g r -> p (g r)").bitcast(FP8X4),
-                    scales=x_scales[:, t].rearrange("p g r -> p (g r)"),
-                    in_=grouped[:].rearrange("p g r j -> p (g r j)"),
-                )
+        def turn(t):
+            turned = turned_pool.tile([P, PASSES * 2, P], F32)
+            for g in range(PASSES):
+                for u in range(2):
+                    nc.tensor.transpose(
+                        turned[:, 2 * g + u, :],
+                        x_words[:, t, PASS_WORDS * g + u : PASS_WORDS * (g + 1) : 2],
+                        identity[:],
+                    )
+            grouped = grouped_pool.tile([P, PASSES, P, PACK], BF16, align_bytes=64)
+            nc.vector.tensor_copy(
+                out=grouped[:].bitcast(F32),
+                in_=turned[:].rearrange("p (g u) r -> p g r u", u=2),
+            )
+            return grouped
+
+        def quantise(t, grouped):
+            nc.vector.quantize_mx(
+                out=x_codes[:, t].rearrange("p g r -> p (g r)").bitcast(FP8X4),
+                scales=x_scales[:, t].rearrange("p g r -> p (g r)"),
+                in_=grouped[:].rearrange("p g r j -> p (g r j)"),
+            )
 
         def rotate(heads, t):
             front = heads[:, :, 0:ROT]
@@ -187,29 +196,43 @@ def tile_progenattention_pa_kernel(
                 out=pairs, in0=pairs, in1=swapped[:].rearrange("p h e j -> p h j e"), op=ALU.add
             )
 
-        quantise_two_tiles(0)
-        for t in range(TILES):
-            result = result_pool.tile([P, OUTPUTS, WIDTH], F32)
-            for o in range(OUTPUTS):
-                for half in range(HALVES):
-                    product = product_pool.tile([P, BANK], F32)
-                    for g in range(PASSES):
-                        nc.tensor.matmul_mx(
-                            out=product[:],
-                            lhsT=x_codes[:, t, g, :].bitcast(FP8X4),
-                            lhsT_scale=x_scales[:, t, g, :],
-                            rhs=w_words[:, g, o, 2 * BANK * half : 2 * BANK * (half + 1)].bitcast(
-                                FP4X4
-                            ),
-                            rhs_scale=w_scales[:, g, o, BANK * half : BANK * (half + 1)],
-                            start=(g == 0),
-                            stop=(g == PASSES - 1),
-                        )
-                    nc.scalar.copy(
-                        out=result[:, o, BANK * half : BANK * (half + 1)], in_=product[:]
+        def multiply(t, o, result):
+            for half in range(HALVES):
+                product = product_pool.tile([P, BANK], F32)
+                for g in range(PASSES):
+                    nc.tensor.matmul_mx(
+                        out=product[:],
+                        lhsT=x_codes[:, t, g, :].bitcast(FP8X4),
+                        lhsT_scale=x_scales[:, t, g, :],
+                        rhs=w_words[:, g, o, 2 * BANK * half : 2 * BANK * (half + 1)].bitcast(FP4X4),
+                        rhs_scale=w_scales[:, g, o, BANK * half : BANK * (half + 1)],
+                        start=(g == 0),
+                        stop=(g == PASSES - 1),
                     )
-                if o < ROTATED:
-                    rotate(result[:, o, :].rearrange("p (h d) -> p h d", d=HEAD), t)
-                nc.sync.dma_start(out=out_hbm[o][:, t, :], in_=result[:, o, :])
-            if t % 2 == 0 and t + 2 < TILES:
-                quantise_two_tiles(t + 2)
+                nc.scalar.copy(out=result[:, o, BANK * half : BANK * (half + 1)], in_=product[:])
+
+        grouped_0 = turn(0)
+        quantise(0, grouped_0)
+        move_w_scales(0)
+        grouped_1 = turn(1)
+        quantise(1, grouped_1)
+        move_w_scales(1)
+        move_w_scales(2)
+
+        for first in range(0, TILES, 2):
+            two_tiles = (first, first + 1)
+            results = []
+            for t in two_tiles:
+                result = result_pool.tile([P, OUTPUTS, WIDTH], F32)
+                results.append(result)
+            for o in range(OUTPUTS):
+                for t, result in zip(two_tiles, results):
+                    multiply(t, o, result)
+                    if o < ROTATED:
+                        rotate(result[:, o, :].rearrange("p (h d) -> p h d", d=HEAD), t)
+                    nc.sync.dma_start(out=out_hbm[o][:, t, :], in_=result[:, o, :])
+                if o == 0 and first + 2 < TILES:
+                    grouped_a = turn(first + 2)
+                    grouped_b = turn(first + 3)
+                    quantise(first + 2, grouped_a)
+                    quantise(first + 3, grouped_b)

@@ -21,7 +21,10 @@ FEATURES = 1024
 PASSES = FEATURES // (P * PACK)
 TILES = TOKENS // P
 OUTPUTS = 3
-ROTATED = 2
+Q_OUT = 0
+K_OUT = 1
+V_OUT = 2
+ORDER = (Q_OUT, V_OUT, K_OUT)
 WIDTH = 1024
 GROUPS = 4
 GROUP_COLS = WIDTH // GROUPS
@@ -86,10 +89,10 @@ def tile_progenattention_pa_kernel(
                 .bitcast(I32)
                 .rearrange("g r n -> r g n"),
             )
-        load_w_words(0)
-        load_w_words(1)
+        load_w_words(ORDER[0])
+        load_w_words(ORDER[1])
         load_x(2, 2, nc.sync)
-        load_w_words(2)
+        load_w_words(ORDER[2])
         load_x(4, 2, nc.sync)
         load_x(6, 2, nc.sync)
 
@@ -213,11 +216,11 @@ def tile_progenattention_pa_kernel(
 
         grouped_0 = turn(0)
         quantise(0, grouped_0)
-        move_w_scales(0)
+        move_w_scales(ORDER[0])
         grouped_1 = turn(1)
         quantise(1, grouped_1)
-        move_w_scales(1)
-        move_w_scales(2)
+        move_w_scales(ORDER[1])
+        move_w_scales(ORDER[2])
 
         for first in range(0, TILES, 2):
             two_tiles = (first, first + 1)
@@ -225,13 +228,13 @@ def tile_progenattention_pa_kernel(
             for t in two_tiles:
                 result = result_pool.tile([P, OUTPUTS, WIDTH], F32)
                 results.append(result)
-            for o in range(OUTPUTS):
+            for o in ORDER:
                 for t, result in zip(two_tiles, results):
                     multiply(t, o, result)
-                    if o < ROTATED:
+                    if o != V_OUT:
                         rotate(result[:, o, :].rearrange("p (h d) -> p h d", d=HEAD), t)
                     nc.sync.dma_start(out=out_hbm[o][:, t, :], in_=result[:, o, :])
-                if o == 0 and first + 2 < TILES:
+                if o == V_OUT and first + 2 < TILES:
                     grouped_a = turn(first + 2)
                     grouped_b = turn(first + 3)
                     quantise(first + 2, grouped_a)

@@ -36,6 +36,8 @@ ROT = 32
 PAIRS = ROT // 2
 WORDS = FEATURES // 2
 PASS_WORDS = WORDS // PASSES
+BUSY_BEFORE_X = 3
+BUSY_BEFORE_W = 4
 ROUND_MAGIC = 12582912.0
 
 FLOPS = 2 * TOKENS * FEATURES * OUTPUTS * WIDTH
@@ -61,9 +63,12 @@ def tile_progenattention_pa_kernel(
         x_codes = keep.tile([P, TILES, PASSES, P], U32, align_bytes=64)
         x_scales = keep.tile([P, TILES, PASSES, P], U8, align_bytes=64)
         w_words = keep.tile([P, PASSES, OUTPUTS, 2 * WIDTH], U8, align_bytes=64)
-        w_scales = keep.tile([P, PASSES, OUTPUTS, WIDTH], U8, align_bytes=64)
+        w_scales = keep.tile([P, OUTPUTS, PASSES, WIDTH], U8, align_bytes=64)
         w_scales_raw = keep.tile([P, PASSES, OUTPUTS * WIDTH], U8)
         identity = keep.tile([P, P], F32)
+        zeros = keep.tile([P, BANK], BF16)
+
+        nc.gpsimd.memset(zeros[:], 0.0)
 
         def load_x(first, count, queue):
             queue.dma_start(
@@ -96,14 +101,16 @@ def tile_progenattention_pa_kernel(
         load_x(4, 2, nc.sync)
         load_x(6, 2, nc.sync)
 
-        position_int = keep.tile([P, TILES], I32)
-        nc.gpsimd.iota(position_int[:], pattern=[[1, TILES]], base=0, channel_multiplier=TILES)
-        make_identity(nc, identity[:])
-        nc.vector.tensor_single_scalar(
-            out=position_int[:], in_=position_int[:], scalar=POSITIONS - 1, op=ALU.bitwise_and
-        )
         position = keep.tile([P, TILES], F32)
-        nc.vector.tensor_copy(out=position[:], in_=position_int[:])
+        for b in range(TOKENS // POSITIONS):
+            nc.gpsimd.iota(
+                position[P // 2 * b : P // 2 * (b + 1), :],
+                pattern=[[1, TILES]],
+                base=0,
+                channel_multiplier=TILES,
+                allow_small_or_imprecise_dtypes=True,
+            )
+        make_identity(nc, identity[:])
         turns = keep.tile([P, TILES, PAIRS], F32)
         for j in range(PAIRS):
             nc.vector.tensor_scalar_mul(
@@ -123,28 +130,35 @@ def tile_progenattention_pa_kernel(
         part = keep.tile([P, TILES, PAIRS], F32)
         nc.vector.tensor_sub(out=part[:], in0=turns[:], in1=whole[:])
         quarter_less = keep.tile([P, TILES, PAIRS], F32)
-        nc.vector.scalar_tensor_tensor(
-            out=quarter_less[:], in0=part[:], scalar=-1.0, in1=part[:], op0=ALU.mult, op1=ALU.min
-        )
-        nc.vector.tensor_scalar_add(out=quarter_less[:], in0=quarter_less[:], scalar1=0.25)
         sin_signed = keep.tile([P, TILES, 2, PAIRS], F32)
         cos_twice = keep.tile([P, TILES, PAIRS, 2], F32)
-        nc.scalar.activation(
-            out=sin_signed[:, :, 0, :], in_=part[:], func=SIN, scale=-2.0 * math.pi
-        )
-        nc.scalar.activation(
-            out=sin_signed[:, :, 1, :], in_=part[:], func=SIN, scale=2.0 * math.pi
-        )
-        nc.scalar.activation(
-            out=cos_twice[:],
-            in_=quarter_less[:].unsqueeze(3).to_broadcast([P, TILES, PAIRS, 2]),
-            func=SIN,
-            scale=2.0 * math.pi,
-        )
+
+        def finish_tables():
+            nc.vector.scalar_tensor_tensor(
+                out=quarter_less[:],
+                in0=part[:],
+                scalar=-1.0,
+                in1=part[:],
+                op0=ALU.mult,
+                op1=ALU.min,
+            )
+            nc.vector.tensor_scalar_add(out=quarter_less[:], in0=quarter_less[:], scalar1=0.25)
+            nc.scalar.activation(
+                out=sin_signed[:, :, 0, :], in_=part[:], func=SIN, scale=-2.0 * math.pi
+            )
+            nc.scalar.activation(
+                out=sin_signed[:, :, 1, :], in_=part[:], func=SIN, scale=2.0 * math.pi
+            )
+            nc.scalar.activation(
+                out=cos_twice[:],
+                in_=quarter_less[:].unsqueeze(3).to_broadcast([P, TILES, PAIRS, 2]),
+                func=SIN,
+                scale=2.0 * math.pi,
+            )
 
         def move_w_scales(o):
             nc.vector.tensor_copy(
-                out=w_scales[:, :, o, :].bitcast(I32).rearrange("p g (m c) -> p g m c", m=GROUPS),
+                out=w_scales[:, o, :, :].bitcast(I32).rearrange("p g (m c) -> p g m c", m=GROUPS),
                 in_=w_scales_raw[:]
                 .bitcast(I32)
                 .rearrange("p g (m o c) -> p g m o c", m=GROUPS, o=OUTPUTS)[:, :, :, o, :],
@@ -208,16 +222,26 @@ def tile_progenattention_pa_kernel(
                         lhsT=x_codes[:, t, g, :].bitcast(FP8X4),
                         lhsT_scale=x_scales[:, t, g, :],
                         rhs=w_words[:, g, o, 2 * BANK * half : 2 * BANK * (half + 1)].bitcast(FP4X4),
-                        rhs_scale=w_scales[:, g, o, BANK * half : BANK * (half + 1)],
+                        rhs_scale=w_scales[:, o, g, BANK * half : BANK * (half + 1)],
                         start=(g == 0),
                         stop=(g == PASSES - 1),
                     )
                 nc.scalar.copy(out=result[:, o, BANK * half : BANK * (half + 1)], in_=product[:])
 
+        def keep_busy(count):
+            for i in range(count):
+                product = product_pool.tile([P, BANK], F32)
+                nc.tensor.matmul(
+                    out=product[:], lhsT=zeros[:, 0:P], rhs=zeros[:], start=True, stop=True
+                )
+
+        keep_busy(BUSY_BEFORE_X)
         grouped_0 = turn(0)
         quantise(0, grouped_0)
         move_w_scales(ORDER[0])
+        finish_tables()
         grouped_1 = turn(1)
+        keep_busy(BUSY_BEFORE_W)
         quantise(1, grouped_1)
         move_w_scales(ORDER[1])
         move_w_scales(ORDER[2])

@@ -191,16 +191,17 @@ def tile_progenattention_pa_kernel(
 
         def rotate(heads, t):
             front = heads[:, :, 0:ROT]
-            swapped = swap_pool.tile([P, HEADS, 2, PAIRS], F32)
+            swapped = swap_pool.tile([P, 2, HEADS, PAIRS], F32)
             for e in range(2):
                 nc.vector.tensor_tensor(
-                    out=swapped[:, :, e, :],
+                    out=swapped[:, e, :, :],
                     in0=heads[:, :, 1 - e : ROT : 2],
                     in1=sin_signed[:, t, e, :].unsqueeze(1).to_broadcast([P, HEADS, PAIRS]),
                     op=ALU.mult,
                 )
+            straight = swap_pool.tile([P, HEADS, ROT], F32)
             nc.vector.tensor_tensor(
-                out=front,
+                out=straight[:],
                 in0=front,
                 in1=cos_twice[:, t]
                 .rearrange("p j e -> p (j e)")
@@ -208,9 +209,11 @@ def tile_progenattention_pa_kernel(
                 .to_broadcast([P, HEADS, ROT]),
                 op=ALU.mult,
             )
-            pairs = front.rearrange("p h (j e) -> p h j e", e=2)
             nc.vector.tensor_tensor(
-                out=pairs, in0=pairs, in1=swapped[:].rearrange("p h e j -> p h j e"), op=ALU.add
+                out=front.rearrange("p h (j e) -> p h j e", e=2),
+                in0=straight[:].rearrange("p h (j e) -> p h j e", e=2),
+                in1=swapped[:].rearrange("p e h j -> p h j e"),
+                op=ALU.add,
             )
 
         def multiply(t, o, result):

@@ -63,8 +63,8 @@ def tile_progenattention_pa_kernel(
         x_codes = keep.tile([P, TILES, PASSES, P], U32, align_bytes=64)
         x_scales = keep.tile([P, TILES, PASSES, P], U8, align_bytes=64)
         w_words = keep.tile([P, PASSES, OUTPUTS, 2 * WIDTH], U8, align_bytes=64)
-        w_scales = keep.tile([P, OUTPUTS, PASSES, WIDTH], U8, align_bytes=64)
-        w_scales_raw = keep.tile([P, PASSES, OUTPUTS * WIDTH], U8)
+        w_scales = keep.tile([P, OUTPUTS, HALVES, PASSES, BANK], U8, align_bytes=64)
+        w_scales_raw = keep.tile([P, HALVES, PASSES, OUTPUTS * BANK], U8)
         identity = keep.tile([P, P], F32)
         zeros = keep.tile([P, BANK], BF16)
 
@@ -75,29 +75,47 @@ def tile_progenattention_pa_kernel(
                 out=x_sb[:, first : first + count, :], in_=x_hbm[:, first : first + count, :]
             )
 
-        def load_w_words(o):
+        def load_w_words(o, first_group, groups):
             for g in range(PASSES):
                 nc.sync.dma_start(
-                    out=w_words[:, g, o, :].bitcast(I32).rearrange("p (m c) -> p m c", m=GROUPS),
+                    out=w_words[
+                        :,
+                        g,
+                        o,
+                        2 * GROUP_COLS * first_group : 2 * GROUP_COLS * (first_group + groups),
+                    ]
+                    .bitcast(I32)
+                    .rearrange("p (m c) -> p m c", m=groups),
                     in_=W_qkv_words[g]
                     .bitcast(I32)
-                    .rearrange("p (m o c) -> p m o c", m=GROUPS, o=OUTPUTS)[:, :, o, :],
+                    .rearrange("p (m o c) -> p m o c", m=GROUPS, o=OUTPUTS)[
+                        :, first_group : first_group + groups, o, :
+                    ],
+                )
+
+        def load_w_scales(half):
+            for quadrant in range(4):
+                nc.sync.dma_start(
+                    out=w_scales_raw[32 * quadrant : 32 * quadrant + 4, half].bitcast(I32),
+                    in_=W_qkv_scales[
+                        :,
+                        4 * quadrant : 4 * quadrant + 4,
+                        OUTPUTS * BANK * half : OUTPUTS * BANK * (half + 1),
+                    ]
+                    .bitcast(I32)
+                    .rearrange("g r n -> r g n"),
                 )
 
         load_x(0, 1, nc.scalar)
         load_x(1, 1, nc.scalar)
-        nc.vector.memset(w_scales_raw[:].bitcast(I32), 0)
-        for quadrant in range(4):
-            nc.sync.dma_start(
-                out=w_scales_raw[32 * quadrant : 32 * quadrant + 4, :, :].bitcast(I32),
-                in_=W_qkv_scales[:, 4 * quadrant : 4 * quadrant + 4, :]
-                .bitcast(I32)
-                .rearrange("g r n -> r g n"),
-            )
-        load_w_words(ORDER[0])
-        load_w_words(ORDER[1])
+        for half in range(HALVES):
+            nc.vector.memset(w_scales_raw[:, half].bitcast(I32), 0)
+        for half in range(HALVES):
+            load_w_scales(half)
+            load_w_words(ORDER[0], GROUPS // HALVES * half, GROUPS // HALVES)
+        load_w_words(ORDER[1], 0, GROUPS)
         load_x(2, 2, nc.sync)
-        load_w_words(ORDER[2])
+        load_w_words(ORDER[2], 0, GROUPS)
         load_x(4, 2, nc.sync)
         load_x(6, 2, nc.sync)
 
@@ -156,12 +174,16 @@ def tile_progenattention_pa_kernel(
                 scale=2.0 * math.pi,
             )
 
-        def move_w_scales(o):
+        def move_w_scales(o, half):
             nc.vector.tensor_copy(
-                out=w_scales[:, o, :, :].bitcast(I32).rearrange("p g (m c) -> p g m c", m=GROUPS),
-                in_=w_scales_raw[:]
+                out=w_scales[:, o, half]
                 .bitcast(I32)
-                .rearrange("p g (m o c) -> p g m o c", m=GROUPS, o=OUTPUTS)[:, :, :, o, :],
+                .rearrange("p g (m c) -> p g m c", m=GROUPS // HALVES),
+                in_=w_scales_raw[:, half]
+                .bitcast(I32)
+                .rearrange("p g (m o c) -> p g m o c", m=GROUPS // HALVES, o=OUTPUTS)[
+                    :, :, :, o, :
+                ],
             )
 
         x_words = x_sb[:].bitcast(F32)
@@ -216,20 +238,19 @@ def tile_progenattention_pa_kernel(
                 op=ALU.add,
             )
 
-        def multiply(t, o, result):
-            for half in range(HALVES):
-                product = product_pool.tile([P, BANK], F32)
-                for g in range(PASSES):
-                    nc.tensor.matmul_mx(
-                        out=product[:],
-                        lhsT=x_codes[:, t, g, :].bitcast(FP8X4),
-                        lhsT_scale=x_scales[:, t, g, :],
-                        rhs=w_words[:, g, o, 2 * BANK * half : 2 * BANK * (half + 1)].bitcast(FP4X4),
-                        rhs_scale=w_scales[:, o, g, BANK * half : BANK * (half + 1)],
-                        start=(g == 0),
-                        stop=(g == PASSES - 1),
-                    )
-                nc.scalar.copy(out=result[:, o, BANK * half : BANK * (half + 1)], in_=product[:])
+        def multiply(t, o, half, result):
+            product = product_pool.tile([P, BANK], F32)
+            for g in range(PASSES):
+                nc.tensor.matmul_mx(
+                    out=product[:],
+                    lhsT=x_codes[:, t, g, :].bitcast(FP8X4),
+                    lhsT_scale=x_scales[:, t, g, :],
+                    rhs=w_words[:, g, o, 2 * BANK * half : 2 * BANK * (half + 1)].bitcast(FP4X4),
+                    rhs_scale=w_scales[:, o, half, g, :],
+                    start=(g == 0),
+                    stop=(g == PASSES - 1),
+                )
+            nc.scalar.copy(out=result[:, o, BANK * half : BANK * (half + 1)], in_=product[:])
 
         def keep_busy(count):
             for i in range(count):
@@ -241,13 +262,15 @@ def tile_progenattention_pa_kernel(
         keep_busy(BUSY_BEFORE_X)
         grouped_0 = turn(0)
         quantise(0, grouped_0)
-        move_w_scales(ORDER[0])
+        move_w_scales(ORDER[0], 0)
         finish_tables()
         grouped_1 = turn(1)
         keep_busy(BUSY_BEFORE_W)
         quantise(1, grouped_1)
-        move_w_scales(ORDER[1])
-        move_w_scales(ORDER[2])
+        move_w_scales(ORDER[0], 1)
+        for o in ORDER[1:]:
+            for half in range(HALVES):
+                move_w_scales(o, half)
 
         for first in range(0, TILES, 2):
             two_tiles = (first, first + 1)
@@ -256,8 +279,13 @@ def tile_progenattention_pa_kernel(
                 result = result_pool.tile([P, OUTPUTS, WIDTH], F32)
                 results.append(result)
             for o in ORDER:
+                if first == 0 and o == ORDER[0]:
+                    for t, result in zip(two_tiles, results):
+                        multiply(t, o, 0, result)
                 for t, result in zip(two_tiles, results):
-                    multiply(t, o, result)
+                    if first > 0 or o != ORDER[0]:
+                        multiply(t, o, 0, result)
+                    multiply(t, o, 1, result)
                     if o != V_OUT:
                         rotate(result[:, o, :].rearrange("p (h d) -> p h d", d=HEAD), t)
                     nc.sync.dma_start(out=out_hbm[o][:, t, :], in_=result[:, o, :])

@@ -32,6 +32,7 @@ BANK = 512
 HALVES = WIDTH // BANK
 HEADS = 8
 HEAD = 128
+BANK_HEADS = BANK // HEAD
 ROT = 32
 PAIRS = ROT // 2
 WORDS = FEATURES // 2
@@ -113,8 +114,8 @@ def tile_progenattention_pa_kernel(
         for half in range(HALVES):
             load_w_scales(half)
             load_w_words(ORDER[0], GROUPS // HALVES * half, GROUPS // HALVES)
-        load_w_words(ORDER[1], 0, GROUPS)
         load_x(2, 2, nc.sync)
+        load_w_words(ORDER[1], 0, GROUPS)
         load_w_words(ORDER[2], 0, GROUPS)
         load_x(4, 2, nc.sync)
         load_x(6, 2, nc.sync)
@@ -211,32 +212,7 @@ def tile_progenattention_pa_kernel(
                 in_=grouped[:].rearrange("p g r j -> p (g r j)"),
             )
 
-        def rotate(heads, t):
-            front = heads[:, :, 0:ROT]
-            swapped = swap_pool.tile([P, 2, HEADS, PAIRS], F32)
-            for e in range(2):
-                nc.vector.tensor_tensor(
-                    out=swapped[:, e, :, :],
-                    in0=heads[:, :, 1 - e : ROT : 2],
-                    in1=sin_signed[:, t, e, :].unsqueeze(1).to_broadcast([P, HEADS, PAIRS]),
-                    op=ALU.mult,
-                )
-            straight = swap_pool.tile([P, HEADS, ROT], F32)
-            nc.vector.tensor_tensor(
-                out=straight[:],
-                in0=front,
-                in1=cos_twice[:, t]
-                .rearrange("p j e -> p (j e)")
-                .unsqueeze(1)
-                .to_broadcast([P, HEADS, ROT]),
-                op=ALU.mult,
-            )
-            nc.vector.tensor_tensor(
-                out=front.rearrange("p h (j e) -> p h j e", e=2),
-                in0=straight[:].rearrange("p h (j e) -> p h j e", e=2),
-                in1=swapped[:].rearrange("p e h j -> p h j e"),
-                op=ALU.add,
-            )
+        products = {}
 
         def multiply(t, o, half, result):
             product = product_pool.tile([P, BANK], F32)
@@ -250,7 +226,45 @@ def tile_progenattention_pa_kernel(
                     start=(g == 0),
                     stop=(g == PASSES - 1),
                 )
-            nc.scalar.copy(out=result[:, o, BANK * half : BANK * (half + 1)], in_=product[:])
+            columns = result[:, o, BANK * half : BANK * (half + 1)]
+            if o == V_OUT:
+                nc.scalar.copy(out=columns, in_=product[:])
+                return
+            if half == 0:
+                swapped = swap_pool.tile([P, 2, HEADS, PAIRS], F32)
+                straight = swap_pool.tile([P, HEADS, ROT], F32)
+                products[(t, o)] = (swapped, straight)
+            swapped, straight = products[(t, o)]
+            sums = product[:].rearrange("p (h d) -> p h d", d=HEAD)
+            these = slice(BANK_HEADS * half, BANK_HEADS * (half + 1))
+            nc.scalar.copy(
+                out=columns.rearrange("p (h d) -> p h d", d=HEAD)[:, :, ROT:HEAD],
+                in_=sums[:, :, ROT:HEAD],
+            )
+            for e in range(2):
+                nc.vector.tensor_tensor(
+                    out=swapped[:, e, these, :],
+                    in0=sums[:, :, 1 - e : ROT : 2],
+                    in1=sin_signed[:, t, e, :].unsqueeze(1).to_broadcast([P, BANK_HEADS, PAIRS]),
+                    op=ALU.mult,
+                )
+            nc.vector.tensor_tensor(
+                out=straight[:, these, :],
+                in0=sums[:, :, 0:ROT],
+                in1=cos_twice[:, t]
+                .rearrange("p j e -> p (j e)")
+                .unsqueeze(1)
+                .to_broadcast([P, BANK_HEADS, ROT]),
+                op=ALU.mult,
+            )
+            if half == HALVES - 1:
+                front = result[:, o, :].rearrange("p (h d) -> p h d", d=HEAD)[:, :, 0:ROT]
+                nc.vector.tensor_tensor(
+                    out=front.rearrange("p h (j e) -> p h j e", e=2),
+                    in0=straight[:].rearrange("p h (j e) -> p h j e", e=2),
+                    in1=swapped[:].rearrange("p e h j -> p h j e"),
+                    op=ALU.add,
+                )
 
         def keep_busy(count):
             for i in range(count):
@@ -286,10 +300,8 @@ def tile_progenattention_pa_kernel(
                     if first > 0 or o != ORDER[0]:
                         multiply(t, o, 0, result)
                     multiply(t, o, 1, result)
-                    if o != V_OUT:
-                        rotate(result[:, o, :].rearrange("p (h d) -> p h d", d=HEAD), t)
                     nc.sync.dma_start(out=out_hbm[o][:, t, :], in_=result[:, o, :])
-                if o == V_OUT and first + 2 < TILES:
+                if o == Q_OUT and first + 2 < TILES:
                     grouped_a = turn(first + 2)
                     grouped_b = turn(first + 3)
                     quantise(first + 2, grouped_a)

@@ -95,16 +95,14 @@ def tile_progenattention_pa_kernel(
                 )
 
         def load_w_scales(half):
-            for quadrant in range(4):
+            for r in range(4):
                 nc.sync.dma_start(
-                    out=w_scales_raw[32 * quadrant : 32 * quadrant + 4, half].bitcast(I32),
+                    out=w_scales_raw[r:P:32, half].bitcast(I32),
                     in_=W_qkv_scales[
-                        :,
-                        4 * quadrant : 4 * quadrant + 4,
-                        OUTPUTS * BANK * half : OUTPUTS * BANK * (half + 1),
+                        :, r:16:4, OUTPUTS * BANK * half : OUTPUTS * BANK * (half + 1)
                     ]
                     .bitcast(I32)
-                    .rearrange("g r n -> r g n"),
+                    .rearrange("g q n -> q g n"),
                 )
 
         load_x(0, 1, nc.scalar)

@@ -54,6 +54,8 @@ def tile_progenattention_pa_kernel(
     ]
 
     with tc.manual_schedule(), tc.tile_pool(name="keep", bufs=1) as keep, tc.tile_pool(
+        name="apart_pool", bufs=2
+    ) as apart_pool, tc.tile_pool(
         name="grouped_pool", bufs=4
     ) as grouped_pool, tc.tile_pool(name="result_pool", bufs=4) as result_pool, tc.tile_pool(
         name="swap_pool", bufs=2
@@ -187,15 +189,25 @@ def tile_progenattention_pa_kernel(
 
         x_words = x_sb[:].bitcast(F32)
 
+        sorted_words = {}
+
+        def sort_words(t):
+            apart = apart_pool.tile([P, PASSES, 2, P], I32)
+            nc.vector.tensor_copy(
+                out=apart[:],
+                in_=x_sb[:, t].bitcast(I32).rearrange("p (g w u) -> p g u w", g=PASSES, u=2),
+            )
+            sorted_words[t] = apart
+
         def turn(t):
             turned = turned_pool.tile([P, PASSES * 2, P], F32)
             for g in range(PASSES):
                 for u in range(2):
-                    nc.tensor.transpose(
-                        turned[:, 2 * g + u, :],
-                        x_words[:, t, PASS_WORDS * g + u : PASS_WORDS * (g + 1) : 2],
-                        identity[:],
-                    )
+                    if t in sorted_words:
+                        words = sorted_words[t][:, g, u, :].bitcast(F32)
+                    else:
+                        words = x_words[:, t, PASS_WORDS * g + u : PASS_WORDS * (g + 1) : 2]
+                    nc.tensor.transpose(turned[:, 2 * g + u, :], words, identity[:])
             grouped = grouped_pool.tile([P, PASSES, P, PACK], BF16, align_bytes=64)
             nc.vector.tensor_copy(
                 out=grouped[:].bitcast(F32),
@@ -235,10 +247,6 @@ def tile_progenattention_pa_kernel(
             swapped, straight = products[(t, o)]
             sums = product[:].rearrange("p (h d) -> p h d", d=HEAD)
             these = slice(BANK_HEADS * half, BANK_HEADS * (half + 1))
-            nc.scalar.copy(
-                out=columns.rearrange("p (h d) -> p h d", d=HEAD)[:, :, ROT:HEAD],
-                in_=sums[:, :, ROT:HEAD],
-            )
             for e in range(2):
                 nc.vector.tensor_tensor(
                     out=swapped[:, e, these, :],
@@ -254,6 +262,10 @@ def tile_progenattention_pa_kernel(
                 .unsqueeze(1)
                 .to_broadcast([P, BANK_HEADS, ROT]),
                 op=ALU.mult,
+            )
+            nc.scalar.copy(
+                out=columns.rearrange("p (h d) -> p h d", d=HEAD)[:, :, ROT:HEAD],
+                in_=sums[:, :, ROT:HEAD],
             )
             if half == HALVES - 1:
                 front = result[:, o, :].rearrange("p (h d) -> p h d", d=HEAD)[:, :, 0:ROT]
@@ -304,3 +316,5 @@ def tile_progenattention_pa_kernel(
                     grouped_b = turn(first + 3)
                     quantise(first + 2, grouped_a)
                     quantise(first + 3, grouped_b)
+            for t in range(first + 4, min(first + 6, TILES)):
+                sort_words(t)

import math

import concourse.mybir as mybir
from concourse.masks import make_identity

F32 = mybir.dt.float32
BF16 = mybir.dt.bfloat16
I32 = mybir.dt.int32
U32 = mybir.dt.uint32
U8 = mybir.dt.uint8
FP8X4 = mybir.dt.float8_e4m3fn_x4
FP4X4 = mybir.dt.float4_e2m1fn_x4
ALU = mybir.AluOpType
SIN = mybir.ActivationFunctionType.Sin

P = 128
PACK = 4
TOKENS = 1024
POSITIONS = 512
FEATURES = 1024
PASSES = FEATURES // (P * PACK)
TILES = TOKENS // P
OUTPUTS = 3
Q_OUT = 0
K_OUT = 1
V_OUT = 2
ORDER = (Q_OUT, V_OUT, K_OUT)
WIDTH = 1024
GROUPS = 4
GROUP_COLS = WIDTH // GROUPS
BANK = 512
HALVES = WIDTH // BANK
HEADS = 8
HEAD = 128
BANK_HEADS = BANK // HEAD
ROT = 32
PAIRS = ROT // 2
WORDS = FEATURES // 2
PASS_WORDS = WORDS // PASSES
BUSY_BEFORE_X = 3
BUSY_BEFORE_W = 4
ROUND_MAGIC = 12582912.0

FLOPS = 2 * TOKENS * FEATURES * OUTPUTS * WIDTH


def tile_progenattention_pa_kernel(
    tc, hidden_states, W_qkv_words, W_qkv_scales, out_0, out_1, out_2
):
    nc = tc.nc
    x_hbm = hidden_states.rearrange("b (q t) e -> (b q) t e", t=TILES)
    out_hbm = [
        o.rearrange("b (q t) h d -> (b q) t (h d)", t=TILES) for o in (out_0, out_1, out_2)
    ]

    with tc.manual_schedule(), tc.tile_pool(name="keep", bufs=1) as keep, tc.tile_pool(
        name="apart_pool", bufs=2
    ) as apart_pool, tc.tile_pool(
        name="grouped_pool", bufs=4
    ) as grouped_pool, tc.tile_pool(name="result_pool", bufs=4) as result_pool, tc.tile_pool(
        name="swap_pool", bufs=2
    ) as swap_pool, tc.psum_pool(name="turned_pool", bufs=2) as turned_pool, tc.psum_pool(
        name="product_pool", bufs=6
    ) as product_pool:
        x_sb = keep.tile([P, TILES, FEATURES], BF16)
        x_codes = keep.tile([P, TILES, PASSES, P], U32, align_bytes=64)
        x_scales = keep.tile([P, TILES, PASSES, P], U8, align_bytes=64)
        w_words = keep.tile([P, PASSES, OUTPUTS, 2 * WIDTH], U8, align_bytes=64)
        w_scales = keep.tile([P, OUTPUTS, HALVES, PASSES, BANK], U8, align_bytes=64)
        w_scales_raw = keep.tile([P, HALVES, PASSES, OUTPUTS * BANK], U8)
        identity = keep.tile([P, P], F32)
        zeros = keep.tile([P, BANK], BF16)

        nc.gpsimd.memset(zeros[:], 0.0)

        def load_x(first, count, queue):
            queue.dma_start(
                out=x_sb[:, first : first + count, :], in_=x_hbm[:, first : first + count, :]
            )

        def load_w_words(o, first_group, groups):
            for g in range(PASSES):
                nc.sync.dma_start(
                    out=w_words[
                        :,
                        g,
                        o,
                        2 * GROUP_COLS * first_group : 2 * GROUP_COLS * (first_group + groups),
                    ]
                    .bitcast(I32)
                    .rearrange("p (m c) -> p m c", m=groups),
                    in_=W_qkv_words[g]
                    .bitcast(I32)
                    .rearrange("p (m o c) -> p m o c", m=GROUPS, o=OUTPUTS)[
                        :, first_group : first_group + groups, o, :
                    ],
                )

        def load_w_scales(half):
            for r in range(4):
                nc.sync.dma_start(
                    out=w_scales_raw[r:P:32, half].bitcast(I32),
                    in_=W_qkv_scales[
                        :, r:16:4, OUTPUTS * BANK * half : OUTPUTS * BANK * (half + 1)
                    ]
                    .bitcast(I32)
                    .rearrange("g q n -> q g n"),
                )

        load_x(0, 1, nc.scalar)
        load_x(1, 1, nc.scalar)
        for half in range(HALVES):
            nc.vector.memset(w_scales_raw[:, half].bitcast(I32), 0)
        for half in range(HALVES):
            load_w_scales(half)
            load_w_words(ORDER[0], GROUPS // HALVES * half, GROUPS // HALVES)
        load_x(2, 2, nc.sync)
        load_w_words(ORDER[1], 0, GROUPS)
        load_w_words(ORDER[2], 0, GROUPS)
        load_x(4, 2, nc.sync)
        load_x(6, 2, nc.sync)

        position = keep.tile([P, TILES], F32)
        for b in range(TOKENS // POSITIONS):
            nc.gpsimd.iota(
                position[P // 2 * b : P // 2 * (b + 1), :],
                pattern=[[1, TILES]],
                base=0,
                channel_multiplier=TILES,
                allow_small_or_imprecise_dtypes=True,
            )
        make_identity(nc, identity[:])
        turns = keep.tile([P, TILES, PAIRS], F32)
        for j in range(PAIRS):
            nc.vector.tensor_scalar_mul(
                out=turns[:, :, j],
                in0=position[:],
                scalar1=10000.0 ** (-j / PAIRS) / (2.0 * math.pi),
            )
        whole = keep.tile([P, TILES, PAIRS], F32)
        nc.vector.tensor_scalar(
            out=whole[:],
            in0=turns[:],
            scalar1=ROUND_MAGIC,
            scalar2=ROUND_MAGIC,
            op0=ALU.add,
            op1=ALU.subtract,
        )
        part = keep.tile([P, TILES, PAIRS], F32)
        nc.vector.tensor_sub(out=part[:], in0=turns[:], in1=whole[:])
        quarter_less = keep.tile([P, TILES, PAIRS], F32)
        sin_signed = keep.tile([P, TILES, 2, PAIRS], F32)
        cos_twice = keep.tile([P, TILES, PAIRS, 2], F32)

        def finish_tables():
            nc.vector.scalar_tensor_tensor(
                out=quarter_less[:],
                in0=part[:],
                scalar=-1.0,
                in1=part[:],
                op0=ALU.mult,
                op1=ALU.min,
            )
            nc.vector.tensor_scalar_add(out=quarter_less[:], in0=quarter_less[:], scalar1=0.25)
            nc.scalar.activation(
                out=sin_signed[:, :, 0, :], in_=part[:], func=SIN, scale=-2.0 * math.pi
            )
            nc.scalar.activation(
                out=sin_signed[:, :, 1, :], in_=part[:], func=SIN, scale=2.0 * math.pi
            )
            nc.scalar.activation(
                out=cos_twice[:],
                in_=quarter_less[:].unsqueeze(3).to_broadcast([P, TILES, PAIRS, 2]),
                func=SIN,
                scale=2.0 * math.pi,
            )

        def move_w_scales(o, half):
            nc.vector.tensor_copy(
                out=w_scales[:, o, half]
                .bitcast(I32)
                .rearrange("p g (m c) -> p g m c", m=GROUPS // HALVES),
                in_=w_scales_raw[:, half]
                .bitcast(I32)
                .rearrange("p g (m o c) -> p g m o c", m=GROUPS // HALVES, o=OUTPUTS)[
                    :, :, :, o, :
                ],
            )

        x_words = x_sb[:].bitcast(F32)

        sorted_words = {}

        def sort_words(t):
            apart = apart_pool.tile([P, PASSES, 2, P], I32)
            nc.vector.tensor_copy(
                out=apart[:],
                in_=x_sb[:, t].bitcast(I32).rearrange("p (g w u) -> p g u w", g=PASSES, u=2),
            )
            sorted_words[t] = apart

        def turn(t):
            turned = turned_pool.tile([P, PASSES * 2, P], F32)
            for g in range(PASSES):
                for u in range(2):
                    if t in sorted_words:
                        words = sorted_words[t][:, g, u, :].bitcast(F32)
                    else:
                        words = x_words[:, t, PASS_WORDS * g + u : PASS_WORDS * (g + 1) : 2]
                    nc.tensor.transpose(turned[:, 2 * g + u, :], words, identity[:])
            grouped = grouped_pool.tile([P, PASSES, P, PACK], BF16, align_bytes=64)
            nc.vector.tensor_copy(
                out=grouped[:].bitcast(F32),
                in_=turned[:].rearrange("p (g u) r -> p g r u", u=2),
            )
            return grouped

        def quantise(t, grouped):
            nc.vector.quantize_mx(
                out=x_codes[:, t].rearrange("p g r -> p (g r)").bitcast(FP8X4),
                scales=x_scales[:, t].rearrange("p g r -> p (g r)"),
                in_=grouped[:].rearrange("p g r j -> p (g r j)"),
            )

        products = {}

        def multiply(t, o, half, result):
            product = product_pool.tile([P, BANK], F32)
            for g in range(PASSES):
                nc.tensor.matmul_mx(
                    out=product[:],
                    lhsT=x_codes[:, t, g, :].bitcast(FP8X4),
                    lhsT_scale=x_scales[:, t, g, :],
                    rhs=w_words[:, g, o, 2 * BANK * half : 2 * BANK * (half + 1)].bitcast(FP4X4),
                    rhs_scale=w_scales[:, o, half, g, :],
                    start=(g == 0),
                    stop=(g == PASSES - 1),
                )
            columns = result[:, o, BANK * half : BANK * (half + 1)]
            if o == V_OUT:
                nc.scalar.copy(out=columns, in_=product[:])
                return
            if half == 0:
                swapped = swap_pool.tile([P, 2, HEADS, PAIRS], F32)
                straight = swap_pool.tile([P, HEADS, ROT], F32)
                products[(t, o)] = (swapped, straight)
            swapped, straight = products[(t, o)]
            sums = product[:].rearrange("p (h d) -> p h d", d=HEAD)
            these = slice(BANK_HEADS * half, BANK_HEADS * (half + 1))
            for e in range(2):
                nc.vector.tensor_tensor(
                    out=swapped[:, e, these, :],
                    in0=sums[:, :, 1 - e : ROT : 2],
                    in1=sin_signed[:, t, e, :].unsqueeze(1).to_broadcast([P, BANK_HEADS, PAIRS]),
                    op=ALU.mult,
                )
            nc.vector.tensor_tensor(
                out=straight[:, these, :],
                in0=sums[:, :, 0:ROT],
                in1=cos_twice[:, t]
                .rearrange("p j e -> p (j e)")
                .unsqueeze(1)
                .to_broadcast([P, BANK_HEADS, ROT]),
                op=ALU.mult,
            )
            nc.scalar.copy(
                out=columns.rearrange("p (h d) -> p h d", d=HEAD)[:, :, ROT:HEAD],
                in_=sums[:, :, ROT:HEAD],
            )
            if half == HALVES - 1:
                front = result[:, o, :].rearrange("p (h d) -> p h d", d=HEAD)[:, :, 0:ROT]
                nc.vector.tensor_tensor(
                    out=front.rearrange("p h (j e) -> p h j e", e=2),
                    in0=straight[:].rearrange("p h (j e) -> p h j e", e=2),
                    in1=swapped[:].rearrange("p e h j -> p h j e"),
                    op=ALU.add,
                )

        def keep_busy(count):
            for i in range(count):
                product = product_pool.tile([P, BANK], F32)
                nc.tensor.matmul(
                    out=product[:], lhsT=zeros[:, 0:P], rhs=zeros[:], start=True, stop=True
                )

        keep_busy(BUSY_BEFORE_X)
        grouped_0 = turn(0)
        quantise(0, grouped_0)
        move_w_scales(ORDER[0], 0)
        finish_tables()
        grouped_1 = turn(1)
        keep_busy(BUSY_BEFORE_W)
        quantise(1, grouped_1)
        move_w_scales(ORDER[0], 1)
        for o in ORDER[1:]:
            for half in range(HALVES):
                move_w_scales(o, half)

        for first in range(0, TILES, 2):
            two_tiles = (first, first + 1)
            results = []
            for t in two_tiles:
                result = result_pool.tile([P, OUTPUTS, WIDTH], F32)
                results.append(result)
            for o in ORDER:
                if first == 0 and o == ORDER[0]:
                    for t, result in zip(two_tiles, results):
                        multiply(t, o, 0, result)
                for t, result in zip(two_tiles, results):
                    if first > 0 or o != ORDER[0]:
                        multiply(t, o, 0, result)
                    multiply(t, o, 1, result)
                    nc.sync.dma_start(out=out_hbm[o][:, t, :], in_=result[:, o, :])
                if o == Q_OUT and first + 2 < TILES:
                    grouped_a = turn(first + 2)
                    grouped_b = turn(first + 3)
                    quantise(first + 2, grouped_a)
                    quantise(first + 3, grouped_b)
            for t in range(first + 4, min(first + 6, TILES)):
                sort_words(t)
